import numpy as np
import ml_dtypes


def mxq(x, axis, fmt="e4m3"):
    dtype, down = {"e4m3": (ml_dtypes.float8_e4m3fn, 7), "e5m2": (ml_dtypes.float8_e5m2, 14)}[fmt]
    v = np.moveaxis(np.asarray(x, np.float32).astype(ml_dtypes.bfloat16).astype(np.float64), axis, -1)
    blocks = v.reshape(v.shape[:-1] + (-1, 32))
    amax = np.abs(blocks).max(-1, keepdims=True)
    byte = np.maximum(np.where(amax > 0, np.frexp(amax)[1] - 1 + 127, 0) - down, 1)
    scale = np.exp2(byte - 127.0)
    codes = (blocks / scale).astype(np.float32).astype(dtype).astype(np.float64)
    return np.moveaxis((codes * scale).reshape(v.shape), -1, axis)


WIDE = False


def mx_kscale(k):
    if not WIDE:
        return np.ones(k)
    levels = np.array([10, -10, 5, -5, 0])
    a = np.random.permutation(np.resize(levels, k // 512 * 4)).reshape(k // 512, 4)
    idx = np.arange(k)
    return np.exp2(a[idx // 512, idx % 128 // 32])


BF16 = ml_dtypes.bfloat16


def bf(x):
    return np.asarray(x, np.float32).astype(BF16)


def f64(x):
    return np.asarray(x).astype(np.float64)


B, H, G, S, D = 8, 8, 2, 512, 128
R = H // G
LAYER_NUMBER = 1
NORM_FACTOR = np.sqrt(D) * LAYER_NUMBER
COEFF = float(LAYER_NUMBER)


def setup_inputs():
    s = mx_kscale(S)
    return {"query_layer": bf(np.random.standard_normal((B, H, S, D)) * 1.5),
            "key_layer": bf(np.random.standard_normal((B, G, S, D))),
            "value_layer": bf(np.random.standard_normal((B, G, S, D)) * (s.max() / s)[:, None]),
            "attention_mask": bf(np.random.standard_normal((B, 1, S, S)) * 0.5 + np.log(s))}


def reference(query_layer, key_layer, value_layer, attention_mask):
    q = f64(query_layer).reshape(B, G, R, S, D)
    k = f64(key_layer)
    scores = q @ k[:, :, None].transpose(0, 1, 2, 4, 3) / NORM_FACTOR
    scores = scores * COEFF
    scores = scores + f64(attention_mask)[:, :, None, :, :]
    e = np.exp(scores - scores.max(-1, keepdims=True))
    out = (mxq(e, 4, "e4m3") @ mxq(f64(value_layer), 2, "e4m3")[:, :, None]) / e.sum(-1, keepdims=True)
    return out.reshape(B, H, S, D)

@@ -1,0 +1,301 @@
+import math
+from contextlib import ExitStack
+
+import concourse.mybir as mybir
+from concourse.masks import make_identity
+
+BF16 = mybir.dt.bfloat16
+F32 = mybir.dt.float32
+U32 = mybir.dt.uint32
+U8 = mybir.dt.uint8
+FP8X4 = mybir.dt.float8_e4m3fn_x4
+ALU = mybir.AluOpType
+ACT = mybir.ActivationFunctionType
+AX = mybir.AxisListType
+
+B, H, G, S, D = 8, 8, 2, 512, 128
+P = 128
+NT = S // P
+NH = B * H
+FLOPS = 2 * 2 * B * H * S * S * D
+
+LT, LC, LQ, LM, LO = 4, 2, 4, 4, 4
+
+
+def tile_selfattention_t_kernel(tc, query_layer, key_layer, value_layer, attention_mask, out):
+    nc = tc.nc
+    c = 1.0 / math.sqrt(D)
+    with ExitStack() as ctx:
+        ctx.enter_context(tc.manual_schedule())
+        const = ctx.enter_context(tc.tile_pool(name="const", bufs=1))
+        loads = ctx.enter_context(tc.tile_pool(name="loads", bufs=2))
+        batch = ctx.enter_context(tc.tile_pool(name="batch", bufs=2))
+        work = ctx.enter_context(tc.tile_pool(name="work", bufs=2))
+        ps_s = ctx.enter_context(tc.psum_pool(name="ps_s", bufs=4))
+        ps_e = ctx.enter_context(tc.psum_pool(name="ps_e", bufs=2))
+        ps_o = ctx.enter_context(tc.psum_pool(name="ps_o", bufs=1))
+        ps_p = ctx.enter_context(tc.psum_pool(name="ps_p", bufs=1))
+
+        ident_b = const.tile([P, P], BF16, name="ident_b")
+        make_identity(nc, ident_b[:])
+        ident_f = const.tile([P, P], F32, name="ident_f")
+        make_identity(nc, ident_f[:])
+
+        k_sb, m_sb, q_sb, v_sb = {}, {}, {}, {}
+        kT, mt, vc, vs = {}, {}, {}, {}
+        qT, sp, e_sb, ep, grp, codes, scales = {}, {}, {}, {}, {}, {}, {}
+        mx, nb, rs = {}, {}, {}
+        prep = {}
+
+        def load_k(b):
+            k_sb[b] = loads.tile([P, G * NT, D], BF16, name="k_sb", tag="k_sb")
+            nc.sync.dma_start(out=k_sb[b][:], in_=key_layer[b].rearrange("g (t p) d -> p (g t) d", p=P))
+
+        def load_m(b):
+            m_sb[b] = loads.tile([P, NT, S], BF16, name="m_sb", tag="m_sb")
+            nc.sync.dma_start(out=m_sb[b][:], in_=attention_mask[b, 0].rearrange("(p j) k -> p j k", j=NT))
+
+        def load_q(b):
+            q_sb[b] = loads.tile([P, H, NT * D], BF16, name="q_sb", tag="q_sb")
+            nc.sync.dma_start(out=q_sb[b][:], in_=query_layer[b].rearrange("h (p j) d -> p h (j d)", j=NT))
+
+        def load_v(b):
+            v_sb[b] = loads.tile([P, G * NT, D], BF16, name="v_sb", tag="v_sb")
+            nc.sync.dma_start(
+                out=v_sb[b][:].rearrange("p (a e) d -> p a (e d)", e=2),
+                in_=value_layer[b].rearrange("g (u p e) d -> p (g u) (e d)", u=2, e=2),
+            )
+
+        def prep_pe(b, i):
+            pt = ps_p.tile([P, 2, NT, P], BF16, name="prep", tag="prep")
+            prep[(b, i)] = pt
+            for a in range(2):
+                for j in range(NT):
+                    if i == 0:
+                        src = k_sb[b][:, a * NT + j, :]
+                    else:
+                        kb = 2 * (i - 1) + a
+                        src = m_sb[b][:, j, kb * P : (kb + 1) * P]
+                    nc.tensor.transpose(out=pt[:, a, j, :], in_=src, identity=ident_b[:])
+
+        def prep_ev(b, i, part, eng):
+            pt = prep[(b, i)]
+            if i == 0:
+                if part == 0:
+                    kT[b] = batch.tile([P, G, S], BF16, name="kT", tag="kT")
+                    dst = kT[b][:].rearrange("p g s -> p (g s)")
+                    src = pt[:].rearrange("p a j i -> p (a j i)")
+                    if eng == "S":
+                        nc.scalar.copy(out=dst, in_=src)
+                    else:
+                        nc.vector.tensor_copy(out=dst, in_=src)
+                return
+            if i == 1 and part == 0:
+                mt[b] = batch.tile([P, NT, NT, P], F32, name="mt", tag="mt")
+            kb = 2 * (i - 1) + part
+            dst = mt[b][:, kb, :, :].rearrange("p j i -> p (j i)")
+            src = pt[:, part, :, :].rearrange("p j i -> p (j i)")
+            if eng == "S":
+                nc.scalar.mul(out=dst, in_=src, mul=math.sqrt(D))
+            else:
+                nc.vector.tensor_scalar_mul(out=dst, in0=src, scalar1=math.sqrt(D))
+
+        def prep_v(b):
+            vg = batch.tile([P, G, D, 4], BF16, name="vg", tag="vg", align_bytes=64)
+            nc.vector.tensor_copy(out=vg[:], in_=v_sb[b][:].rearrange("p (g t) d -> p g d t", g=G))
+            vc[b] = batch.tile([P, G * D], U32, name="vc", tag="vc", align_bytes=64)
+            vs[b] = batch.tile([P, G * D], U8, name="vs", tag="vs", align_bytes=64)
+            nc.vector.quantize_mx(
+                out=vc[b][:].bitcast(FP8X4), scales=vs[b][:], in_=vg[:].rearrange("p g d t -> p (g d t)")
+            )
+
+        def qt_pe(n):
+            pt = ps_p.tile([P, 2, NT, P], BF16, name="prep", tag="prep")
+            prep[("q", n)] = pt
+            for a in range(2):
+                for j in range(NT):
+                    nc.tensor.transpose(
+                        out=pt[:, a, j, :],
+                        in_=q_sb[(n + a) // H][:, (n + a) % H, j * D : (j + 1) * D],
+                        identity=ident_b[:],
+                    )
+
+        def qt_ev(n, eng):
+            qT[n // 2] = work.tile([P, 2, NT, P], BF16, name="qT", tag="qT", bufs=2)
+            dst = qT[n // 2][:].rearrange("p a j i -> p (a j i)")
+            src = prep[("q", n)][:].rearrange("p a j i -> p (a j i)")
+            if eng == "S":
+                nc.scalar.copy(out=dst, in_=src)
+            else:
+                nc.vector.tensor_copy(out=dst, in_=src)
+
+        def qk(t):
+            n, j = t // NT, t % NT
+            b, h = n // H, n % H
+            sp[t] = ps_s.tile([P, S], F32, name="sp", tag="sp")
+            nc.tensor.matmul(
+                out=sp[t][:], lhsT=qT[n // 2][:, n % 2, j, :], rhs=kT[b][:, h // (H // G), :], start=True, stop=False
+            )
+
+        def ta(t):
+            n, j = t // NT, t % NT
+            b = n // H
+            for kb in range(NT):
+                nc.tensor.matmul(
+                    out=sp[t][:, kb * P : (kb + 1) * P],
+                    lhsT=mt[b][:, kb, j, :],
+                    rhs=ident_f[:],
+                    start=False,
+                    stop=(kb == NT - 1),
+                    is_transpose=True,
+                )
+
+        def be(t):
+            n, j = t // NT, t % NT
+            if j == 0:
+                mx[n] = work.tile([P, NT], F32, name="mx", tag="mx", bufs=3)
+                nb[n] = work.tile([P, NT], F32, name="nb", tag="nb", bufs=3)
+                rs[n] = work.tile([P, NT], F32, name="rs", tag="rs", bufs=LO + 3)
+            nc.vector.tensor_reduce(out=mx[n][:, j : j + 1], in_=sp[t][:], axis=AX.X, op=ALU.max)
+            nc.vector.tensor_scalar_mul(out=nb[n][:, j : j + 1], in0=mx[n][:, j : j + 1], scalar1=-c)
+            e_sb[t] = work.tile([P, S], BF16, name="e_sb", tag="e_sb", bufs=10)
+            nc.scalar.activation(
+                out=e_sb[t][:], in_=sp[t][:], func=ACT.Exp, bias=nb[n][:, j : j + 1], scale=c,
+                accum_out=rs[n][:, j : j + 1],
+            )
+
+        def te(t):
+            if t < 0 or t >= NH * NT:
+                return
+            r = t // 2
+            if t % 2 == 0:
+                ep[r] = ps_e.tile([P, 2, 2, P], F32, name="ep", tag="ep")
+            for u in range(2):
+                nc.tensor.transpose(
+                    out=ep[r][:, t % 2, u, :], in_=e_sb[t][:].bitcast(F32)[:, u * P : (u + 1) * P], identity=ident_f[:]
+                )
+
+        def cp(r):
+            if r < 0 or r >= NH * 2:
+                return
+            grp[r] = work.tile([P, 2, P, 4], BF16, name="grp", tag="grp", bufs=5, align_bytes=64)
+            dst = grp[r][:].bitcast(F32)
+            src = ep[r][:].rearrange("p a u i -> p a i u")
+            if 'S' == "S":
+                nc.scalar.copy(out=dst, in_=src)
+            else:
+                nc.vector.tensor_copy(out=dst, in_=src)
+
+        def qz(r):
+            if r < 0 or r >= NH * 2:
+                return
+            codes[r] = work.tile([P, 2 * P], U32, name="codes", tag="codes", bufs=9, align_bytes=64)
+            scales[r] = work.tile([P, 2 * P], U8, name="scales", tag="scales", bufs=9, align_bytes=64)
+            nc.vector.quantize_mx(
+                out=codes[r][:].bitcast(FP8X4), scales=scales[r][:], in_=grp[r][:].rearrange("p a i t -> p (a i t)")
+            )
+
+        o_ps = {}
+
+        def mm(n):
+            if n < 0 or n >= NH:
+                return
+            b, g = n // H, (n % H) // (H // G)
+            o_ps[n] = ps_o.tile([P, NT, D], F32, name="o_ps", tag="o_ps")
+            for j in range(NT):
+                r, a = 2 * n + j // 2, j % 2
+                nc.tensor.matmul_mx(
+                    out=o_ps[n][:, j, :],
+                    lhsT=codes[r][:, a * P : (a + 1) * P].bitcast(FP8X4),
+                    lhsT_scale=scales[r][:, a * P : (a + 1) * P],
+                    rhs=vc[b][:, g * D : (g + 1) * D].bitcast(FP8X4),
+                    rhs_scale=vs[b][:, g * D : (g + 1) * D],
+                    start=True,
+                    stop=True,
+                )
+
+        def ov(n):
+            if n < 0 or n >= NH:
+                return
+            ri = work.tile([P, NT], F32, name="ri", tag="ri", bufs=2)
+            nc.vector.reciprocal(out=ri[:], in_=rs[n][:])
+            o_sb = work.tile([P, NT, D], F32, name="o_sb", tag="o_sb", bufs=4)
+            nc.vector.tensor_tensor(
+                out=o_sb[:], in0=o_ps[n][:], in1=ri[:].unsqueeze(2).to_broadcast([P, NT, D]), op=ALU.mult
+            )
+            nc.sync.dma_start(out=out[n // H, n % H].rearrange("(p j) d -> p j d", j=NT), in_=o_sb[:])
+
+        load_k(0)
+        load_m(0)
+        load_q(0)
+        load_v(0)
+        load_k(1)
+        load_m(1)
+        prep_pe(0, 0)
+        prep_ev(0, 0, 0, "S")
+        prep_pe(0, 1)
+        prep_ev(0, 1, 0, "V")
+        prep_ev(0, 1, 1, "S")
+        prep_pe(0, 2)
+        prep_ev(0, 2, 0, "V")
+        prep_ev(0, 2, 1, "S")
+        qt_pe(0)
+        qt_ev(0, "V")
+        prep_v(0)
+
+        drain = max(LM, LO) + (LT + NT - 1) // NT + 2
+        for n in range(NH + drain):
+            b, hn = n // H, n % H
+            live = n < NH
+            t0 = NT * n
+            if live and hn == 0:
+                if b + 1 < B:
+                    load_q(b + 1)
+                    load_v(b + 1)
+                if b + 2 < B:
+                    load_k(b + 2)
+                    load_m(b + 2)
+            if live:
+                qk(t0)
+                mm(n - LM)
+                qk(t0 + 1)
+                ta(t0)
+                ta(t0 + 1)
+            else:
+                mm(n - LM)
+            te(t0 - LT)
+            te(t0 + 1 - LT)
+            do_qt = hn % 2 == 1 and n + 1 < NH
+            pi = hn // 2 if hn % 2 == 0 else -1
+            do_p = live and b + 1 < B and 0 <= pi < 3
+            if do_qt:
+                qt_pe(n + 1)
+            if do_p:
+                prep_pe(b + 1, pi)
+            ov(n - LO)
+            if live:
+                be(t0)
+                be(t0 + 1)
+            if do_qt:
+                qt_ev(n + 1, "V")
+            if do_p:
+                prep_ev(b + 1, pi, 0, "S")
+            cp(2 * n - LC)
+            qz(2 * n - LQ)
+            if live:
+                qk(t0 + 2)
+                ta(t0 + 2)
+            te(t0 + 2 - LT)
+            if live:
+                qk(t0 + 3)
+                ta(t0 + 3)
+            te(t0 + 3 - LT)
+            if live:
+                be(t0 + 2)
+                if do_p:
+                    prep_ev(b + 1, pi, 1, "S")
+                be(t0 + 3)
+            cp(2 * n + 1 - LC)
+            qz(2 * n + 1 - LQ)
+            if live and b + 1 < B and hn == 6:
+                prep_v(b + 1)

@@ -157,7 +157,7 @@ def tile_selfattention_t_kernel(tc, query_layer, key_layer, value_layer, attenti
                 nb[n] = work.tile([P, NT], F32, name="nb", tag="nb", bufs=3)
                 rs[n] = work.tile([P, NT], F32, name="rs", tag="rs", bufs=LO + 3)
             nc.vector.tensor_reduce(out=mx[n][:, j : j + 1], in_=sp[t][:], axis=AX.X, op=ALU.max)
-            nc.vector.tensor_scalar_mul(out=nb[n][:, j : j + 1], in0=mx[n][:, j : j + 1], scalar1=-c)
+            nc.gpsimd.tensor_scalar(out=nb[n][:, j : j + 1], in0=mx[n][:, j : j + 1], scalar1=-c, scalar2=0.0, op0=ALU.mult, op1=ALU.add)
             e_sb[t] = work.tile([P, S], BF16, name="e_sb", tag="e_sb", bufs=10)
             nc.scalar.activation(
                 out=e_sb[t][:], in_=sp[t][:], func=ACT.Exp, bias=nb[n][:, j : j + 1], scale=c,
@@ -214,14 +214,20 @@ def tile_selfattention_t_kernel(tc, query_layer, key_layer, value_layer, attenti
                     stop=True,
                 )
 
+        ri = {}
+
+        def rc(n):
+            if n < 0 or n >= NH:
+                return
+            ri[n] = work.tile([P, NT], F32, name="ri", tag="ri", bufs=3)
+            nc.vector.reciprocal(out=ri[n][:], in_=rs[n][:])
+
         def ov(n):
             if n < 0 or n >= NH:
                 return
-            ri = work.tile([P, NT], F32, name="ri", tag="ri", bufs=2)
-            nc.vector.reciprocal(out=ri[:], in_=rs[n][:])
             o_sb = work.tile([P, NT, D], F32, name="o_sb", tag="o_sb", bufs=4)
             nc.vector.tensor_tensor(
-                out=o_sb[:], in0=o_ps[n][:], in1=ri[:].unsqueeze(2).to_broadcast([P, NT, D]), op=ALU.mult
+                out=o_sb[:], in0=o_ps[n][:], in1=ri[n][:].unsqueeze(2).to_broadcast([P, NT, D]), op=ALU.mult
             )
             nc.sync.dma_start(out=out[n // H, n % H].rearrange("(p j) d -> p j d", j=NT), in_=o_sb[:])
 
@@ -297,5 +303,6 @@ def tile_selfattention_t_kernel(tc, query_layer, key_layer, value_layer, attenti
                 be(t0 + 3)
             cp(2 * n + 1 - LC)
             qz(2 * n + 1 - LQ)
+            rc(n + 1 - LO)
             if live and b + 1 < B and hn == 6:
                 prep_v(b + 1)

@@ -132,21 +132,21 @@ def tile_selfattention_t_kernel(tc, query_layer, key_layer, value_layer, attenti
         def qk(t):
             n, j = t // NT, t % NT
             b, h = n // H, n % H
-            sp[t] = ps_s.tile([P, S], F32, name="sp", tag="sp")
             nc.tensor.matmul(
-                out=sp[t][:], lhsT=qT[n // 2][:, n % 2, j, :], rhs=kT[b][:, h // (H // G), :], start=True, stop=False
+                out=sp[t][:], lhsT=qT[n // 2][:, n % 2, j, :], rhs=kT[b][:, h // (H // G), :], start=False, stop=True
             )
 
         def ta(t):
             n, j = t // NT, t % NT
             b = n // H
+            sp[t] = ps_s.tile([P, S], F32, name="sp", tag="sp")
             for kb in range(NT):
                 nc.tensor.matmul(
                     out=sp[t][:, kb * P : (kb + 1) * P],
                     lhsT=mt[b][:, kb, j, :],
                     rhs=ident_f[:],
-                    start=False,
-                    stop=(kb == NT - 1),
+                    start=(kb == 0),
+                    stop=False,
                     is_transpose=True,
                 )
 
@@ -262,11 +262,11 @@ def tile_selfattention_t_kernel(tc, query_layer, key_layer, value_layer, attenti
                     load_k(b + 2)
                     load_m(b + 2)
             if live:
+                ta(t0)
+                ta(t0 + 1)
                 qk(t0)
                 mm(n - LM)
                 qk(t0 + 1)
-                ta(t0)
-                ta(t0 + 1)
             else:
                 mm(n - LM)
             te(t0 - LT)
@@ -289,12 +289,12 @@ def tile_selfattention_t_kernel(tc, query_layer, key_layer, value_layer, attenti
             cp(2 * n - LC)
             qz(2 * n - LQ)
             if live:
-                qk(t0 + 2)
                 ta(t0 + 2)
+                qk(t0 + 2)
             te(t0 + 2 - LT)
             if live:
-                qk(t0 + 3)
                 ta(t0 + 3)
+                qk(t0 + 3)
             te(t0 + 3 - LT)
             if live:
                 be(t0 + 2)

@@ -17,9 +17,8 @@ B, H, G, S, D = 8, 8, 2, 512, 128
 P = 128
 NT = S // P
 NH = B * H
+NM = 3
 FLOPS = 2 * 2 * B * H * S * S * D
-
-LT, LC, LQ, LM, LO = 4, 2, 4, 4, 4
 
 
 def tile_selfattention_t_kernel(tc, query_layer, key_layer, value_layer, attention_mask, out):
@@ -43,23 +42,34 @@ def tile_selfattention_t_kernel(tc, query_layer, key_layer, value_layer, attenti
 
         k_sb, m_sb, q_sb, v_sb = {}, {}, {}, {}
         kT, mt, vc, vs = {}, {}, {}, {}
-        qT, sp, e_sb, ep, grp, codes, scales = {}, {}, {}, {}, {}, {}, {}
-        mx, nb, rs = {}, {}, {}
+        qT, sp, s_sb, e_sb, ep, grp, codes, scales = {}, {}, {}, {}, {}, {}, {}, {}
+        mx, nb, nbv, rs, ri, o_ps = {}, {}, {}, {}, {}, {}
         prep = {}
 
+        def live(n):
+            return 0 <= n < NH
+
         def load_k(b):
+            if b >= B:
+                return
             k_sb[b] = loads.tile([P, G * NT, D], BF16, name="k_sb", tag="k_sb")
             nc.sync.dma_start(out=k_sb[b][:], in_=key_layer[b].rearrange("g (t p) d -> p (g t) d", p=P))
 
         def load_m(b):
-            m_sb[b] = loads.tile([P, NT, S], BF16, name="m_sb", tag="m_sb")
+            if b >= B:
+                return
+            m_sb[b] = loads.tile([P, NT, S], BF16, name="m_sb", tag="m_sb", bufs=3)
             nc.sync.dma_start(out=m_sb[b][:], in_=attention_mask[b, 0].rearrange("(p j) k -> p j k", j=NT))
 
         def load_q(b):
+            if b >= B:
+                return
             q_sb[b] = loads.tile([P, H, NT * D], BF16, name="q_sb", tag="q_sb")
             nc.sync.dma_start(out=q_sb[b][:], in_=query_layer[b].rearrange("h (p j) d -> p h (j d)", j=NT))
 
         def load_v(b):
+            if b >= B:
+                return
             v_sb[b] = loads.tile([P, G * NT, D], BF16, name="v_sb", tag="v_sb")
             nc.sync.dma_start(
                 out=v_sb[b][:].rearrange("p (a e) d -> p a (e d)", e=2),
@@ -70,7 +80,7 @@ def tile_selfattention_t_kernel(tc, query_layer, key_layer, value_layer, attenti
             pt = ps_p.tile([P, 2, NT, P], BF16, name="prep", tag="prep")
             prep[(b, i)] = pt
             for a in range(2):
-                for j in range(NT):
+                for j in range(NT if i == 0 else NM):
                     if i == 0:
                         src = k_sb[b][:, a * NT + j, :]
                     else:
@@ -85,16 +95,13 @@ def tile_selfattention_t_kernel(tc, query_layer, key_layer, value_layer, attenti
                     kT[b] = batch.tile([P, G, S], BF16, name="kT", tag="kT")
                     dst = kT[b][:].rearrange("p g s -> p (g s)")
                     src = pt[:].rearrange("p a j i -> p (a j i)")
-                    if eng == "S":
-                        nc.scalar.copy(out=dst, in_=src)
-                    else:
-                        nc.vector.tensor_copy(out=dst, in_=src)
+                    nc.scalar.copy(out=dst, in_=src)
                 return
             if i == 1 and part == 0:
-                mt[b] = batch.tile([P, NT, NT, P], F32, name="mt", tag="mt")
+                mt[b] = batch.tile([P, NT, NM, P], F32, name="mt", tag="mt")
             kb = 2 * (i - 1) + part
             dst = mt[b][:, kb, :, :].rearrange("p j i -> p (j i)")
-            src = pt[:, part, :, :].rearrange("p j i -> p (j i)")
+            src = pt[:, part, 0:NM, :].rearrange("p j i -> p (j i)")
             if eng == "S":
                 nc.scalar.mul(out=dst, in_=src, mul=math.sqrt(D))
             else:
@@ -121,7 +128,7 @@ def tile_selfattention_t_kernel(tc, query_layer, key_layer, value_layer, attenti
                     )
 
         def qt_ev(n, eng):
-            qT[n // 2] = work.tile([P, 2, NT, P], BF16, name="qT", tag="qT", bufs=2)
+            qT[n // 2] = work.tile([P, 2, NT, P], BF16, name="qT", tag="qT", bufs=3)
             dst = qT[n // 2][:].rearrange("p a j i -> p (a j i)")
             src = prep[("q", n)][:].rearrange("p a j i -> p (a j i)")
             if eng == "S":
@@ -129,76 +136,133 @@ def tile_selfattention_t_kernel(tc, query_layer, key_layer, value_layer, attenti
             else:
                 nc.vector.tensor_copy(out=dst, in_=src)
 
-        def qk(t):
-            n, j = t // NT, t % NT
+        def bf(m):
+            if not live(m):
+                return
+            b, hn = m // H, m % H
+            if hn % 2 == 1:
+                if m + 1 < NH:
+                    qt_pe(m + 1)
+            elif b + 1 < B and hn // 2 < 3:
+                prep_pe(b + 1, hn // 2)
+
+        def eva(m):
+            if not live(m):
+                return
+            b, hn = m // H, m % H
+            if hn % 2 == 1:
+                if m + 1 < NH:
+                    qt_ev(m + 1, "S")
+            elif b + 1 < B and hn // 2 < 3:
+                prep_ev(b + 1, hn // 2, 0, "S")
+
+        def evb(m):
+            if not live(m):
+                return
+            b, hn = m // H, m % H
+            if hn % 2 == 0 and b + 1 < B and 1 <= hn // 2 < 3:
+                prep_ev(b + 1, hn // 2, 1, "S")
+
+        def pv(m):
+            if live(m) and m % H == 6 and m // H + 1 < B:
+                prep_v(m // H + 1)
+
+        def qk(n, j):
+            if not live(n):
+                return
+            t = n * NT + j
             b, h = n // H, n % H
+            sp[t] = ps_s.tile([P, S], F32, name="sp", tag="sp")
             nc.tensor.matmul(
-                out=sp[t][:], lhsT=qT[n // 2][:, n % 2, j, :], rhs=kT[b][:, h // (H // G), :], start=False, stop=True
+                out=sp[t][:], lhsT=qT[n // 2][:, n % 2, j, :], rhs=kT[b][:, h // (H // G), :], start=True, stop=(j >= NM)
             )
 
-        def ta(t):
-            n, j = t // NT, t % NT
-            b = n // H
-            sp[t] = ps_s.tile([P, S], F32, name="sp", tag="sp")
+        def ta(n, j):
+            if not live(n):
+                return
+            t = n * NT + j
             for kb in range(NT):
                 nc.tensor.matmul(
                     out=sp[t][:, kb * P : (kb + 1) * P],
-                    lhsT=mt[b][:, kb, j, :],
+                    lhsT=mt[n // H][:, kb, j, :],
                     rhs=ident_f[:],
-                    start=(kb == 0),
-                    stop=False,
+                    start=False,
+                    stop=(kb == NT - 1),
                     is_transpose=True,
                 )
 
-        def be(t):
-            n, j = t // NT, t % NT
-            if j == 0:
-                mx[n] = work.tile([P, NT], F32, name="mx", tag="mx", bufs=3)
-                nb[n] = work.tile([P, NT], F32, name="nb", tag="nb", bufs=3)
-                rs[n] = work.tile([P, NT], F32, name="rs", tag="rs", bufs=LO + 3)
-            nc.vector.tensor_reduce(out=mx[n][:, j : j + 1], in_=sp[t][:], axis=AX.X, op=ALU.max)
-            nc.gpsimd.tensor_scalar(out=nb[n][:, j : j + 1], in0=mx[n][:, j : j + 1], scalar1=-c, scalar2=0.0, op0=ALU.mult, op1=ALU.add)
-            e_sb[t] = work.tile([P, S], BF16, name="e_sb", tag="e_sb", bufs=10)
-            nc.scalar.activation(
-                out=e_sb[t][:], in_=sp[t][:], func=ACT.Exp, bias=nb[n][:, j : j + 1], scale=c,
-                accum_out=rs[n][:, j : j + 1],
+        def stt(n, j):
+            if not live(n):
+                return
+            t = n * NT + j
+            s_sb[t] = work.tile([P, S], F32, name="s_sb", tag="s_sb", bufs=4)
+            nc.vector.scalar_tensor_tensor(
+                out=s_sb[t][:], in0=sp[t][:], scalar=c, in1=m_sb[n // H][:, j, :], op0=ALU.mult, op1=ALU.add
             )
 
-        def te(t):
-            if t < 0 or t >= NH * NT:
+        def red(n, j):
+            if not live(n):
                 return
-            r = t // 2
-            if t % 2 == 0:
-                ep[r] = ps_e.tile([P, 2, 2, P], F32, name="ep", tag="ep")
-            for u in range(2):
-                nc.tensor.transpose(
-                    out=ep[r][:, t % 2, u, :], in_=e_sb[t][:].bitcast(F32)[:, u * P : (u + 1) * P], identity=ident_f[:]
-                )
+            t = n * NT + j
+            if j >= NM:
+                nbv[t] = work.tile([P, 1], F32, name="nbv", tag="nbv", bufs=6)
+                nc.vector.tensor_reduce(out=nbv[t][:], in_=s_sb[t][:], axis=AX.X, op=ALU.max, negate=True)
+                return
+            if n not in mx:
+                mx[n] = work.tile([P, NT], F32, name="mx", tag="mx", bufs=4)
+                nb[n] = work.tile([P, NT], F32, name="nb", tag="nb", bufs=4)
+            nc.vector.tensor_reduce(out=mx[n][:, j : j + 1], in_=sp[t][:], axis=AX.X, op=ALU.max)
+            nc.gpsimd.tensor_scalar(
+                out=nb[n][:, j : j + 1], in0=mx[n][:, j : j + 1], scalar1=-c, scalar2=0.0, op0=ALU.mult, op1=ALU.add
+            )
 
-        def cp(r):
-            if r < 0 or r >= NH * 2:
+        def ex(n, j):
+            if not live(n):
                 return
-            grp[r] = work.tile([P, 2, P, 4], BF16, name="grp", tag="grp", bufs=5, align_bytes=64)
-            dst = grp[r][:].bitcast(F32)
-            src = ep[r][:].rearrange("p a u i -> p a i u")
-            if 'S' == "S":
-                nc.scalar.copy(out=dst, in_=src)
+            t = n * NT + j
+            if n not in rs:
+                rs[n] = work.tile([P, NT], F32, name="rs", tag="rs", bufs=8)
+            e_sb[t] = work.tile([P, S], BF16, name="e_sb", tag="e_sb", bufs=16)
+            if j >= NM:
+                scores, factor, bias = s_sb[t], 1.0, nbv[t][:]
             else:
-                nc.vector.tensor_copy(out=dst, in_=src)
+                scores, factor, bias = sp[t], c, nb[n][:, j : j + 1]
+            nc.scalar.activation(
+                out=e_sb[t][:], in_=scores[:], func=ACT.Exp, bias=bias, scale=factor, accum_out=rs[n][:, j : j + 1]
+            )
 
-        def qz(r):
-            if r < 0 or r >= NH * 2:
+        def te(n, a):
+            if not live(n):
                 return
-            codes[r] = work.tile([P, 2 * P], U32, name="codes", tag="codes", bufs=9, align_bytes=64)
-            scales[r] = work.tile([P, 2 * P], U8, name="scales", tag="scales", bufs=9, align_bytes=64)
+            r = 2 * n + a
+            ep[r] = ps_e.tile([P, 2, 2, P], F32, name="ep", tag="ep")
+            for i in range(2):
+                for u in range(2):
+                    nc.tensor.transpose(
+                        out=ep[r][:, i, u, :],
+                        in_=e_sb[2 * r + i][:].bitcast(F32)[:, u * P : (u + 1) * P],
+                        identity=ident_f[:],
+                    )
+
+        def cp(n, a):
+            if not live(n):
+                return
+            r = 2 * n + a
+            grp[r] = work.tile([P, 2, P, 4], BF16, name="grp", tag="grp", bufs=8, align_bytes=64)
+            nc.scalar.copy(out=grp[r][:].bitcast(F32), in_=ep[r][:].rearrange("p a u i -> p a i u"))
+
+        def qz(n, a):
+            if not live(n):
+                return
+            r = 2 * n + a
+            codes[r] = work.tile([P, 2 * P], U32, name="codes", tag="codes", bufs=12, align_bytes=64)
+            scales[r] = work.tile([P, 2 * P], U8, name="scales", tag="scales", bufs=12, align_bytes=64)
             nc.vector.quantize_mx(
                 out=codes[r][:].bitcast(FP8X4), scales=scales[r][:], in_=grp[r][:].rearrange("p a i t -> p (a i t)")
             )
 
-        o_ps = {}
-
         def mm(n):
-            if n < 0 or n >= NH:
+            if not live(n):
                 return
             b, g = n // H, (n % H) // (H // G)
             o_ps[n] = ps_o.tile([P, NT, D], F32, name="o_ps", tag="o_ps")
@@ -214,16 +278,14 @@ def tile_selfattention_t_kernel(tc, query_layer, key_layer, value_layer, attenti
                     stop=True,
                 )
 
-        ri = {}
-
         def rc(n):
-            if n < 0 or n >= NH:
+            if not live(n):
                 return
-            ri[n] = work.tile([P, NT], F32, name="ri", tag="ri", bufs=3)
+            ri[n] = work.tile([P, NT], F32, name="ri", tag="ri", bufs=4)
             nc.vector.reciprocal(out=ri[n][:], in_=rs[n][:])
 
         def ov(n):
-            if n < 0 or n >= NH:
+            if not live(n):
                 return
             o_sb = work.tile([P, NT, D], F32, name="o_sb", tag="o_sb", bufs=4)
             nc.vector.tensor_tensor(
@@ -249,60 +311,38 @@ def tile_selfattention_t_kernel(tc, query_layer, key_layer, value_layer, attenti
         qt_ev(0, "V")
         prep_v(0)
 
-        drain = max(LM, LO) + (LT + NT - 1) // NT + 2
-        for n in range(NH + drain):
-            b, hn = n // H, n % H
-            live = n < NH
-            t0 = NT * n
-            if live and hn == 0:
-                if b + 1 < B:
-                    load_q(b + 1)
-                    load_v(b + 1)
-                if b + 2 < B:
-                    load_k(b + 2)
-                    load_m(b + 2)
-            if live:
-                ta(t0)
-                ta(t0 + 1)
-                qk(t0)
-                mm(n - LM)
-                qk(t0 + 1)
-            else:
-                mm(n - LM)
-            te(t0 - LT)
-            te(t0 + 1 - LT)
-            do_qt = hn % 2 == 1 and n + 1 < NH
-            pi = hn // 2 if hn % 2 == 0 else -1
-            do_p = live and b + 1 < B and 0 <= pi < 3
-            if do_qt:
-                qt_pe(n + 1)
-            if do_p:
-                prep_pe(b + 1, pi)
-            ov(n - LO)
-            if live:
-                be(t0)
-                be(t0 + 1)
-            if do_qt:
-                qt_ev(n + 1, "V")
-            if do_p:
-                prep_ev(b + 1, pi, 0, "S")
-            cp(2 * n - LC)
-            qz(2 * n - LQ)
-            if live:
-                ta(t0 + 2)
-                qk(t0 + 2)
-            te(t0 + 2 - LT)
-            if live:
-                ta(t0 + 3)
-                qk(t0 + 3)
-            te(t0 + 3 - LT)
-            if live:
-                be(t0 + 2)
-                if do_p:
-                    prep_ev(b + 1, pi, 1, "S")
-                be(t0 + 3)
-            cp(2 * n + 1 - LC)
-            qz(2 * n + 1 - LQ)
-            rc(n + 1 - LO)
-            if live and b + 1 < B and hn == 6:
-                prep_v(b + 1)
+        for n in range(NH + 4):
+            if n < NH and n % H == 0:
+                load_q(n // H + 1)
+                load_v(n // H + 1)
+                load_k(n // H + 2)
+                load_m(n // H + 2)
+            te(n - 2, 1)
+            cp(n - 2, 0)
+            red(n - 1, 2)
+            qz(n - 3, 0)
+            red(n - 1, 3)
+            pv(n - 1)
+            ex(n - 1, 1)
+            cp(n - 2, 1)
+            bf(n)
+            ex(n - 1, 2)
+            qk(n, 0)
+            ta(n, 0)
+            qk(n, 3)
+            mm(n - 4)
+            ex(n - 1, 3)
+            red(n, 0)
+            stt(n, 3)
+            qk(n, 1)
+            ta(n, 1)
+            qz(n - 3, 1)
+            red(n, 1)
+            te(n - 1, 0)
+            eva(n)
+            qk(n, 2)
+            evb(n)
+            ta(n, 2)
+            ov(n - 4)
+            rc(n - 2)
+            ex(n, 0)

@@ -67,6 +67,13 @@ def tile_selfattention_t_kernel(tc, query_layer, key_layer, value_layer, attenti
             q_sb[b] = loads.tile([P, H, NT * D], BF16, name="q_sb", tag="q_sb")
             nc.sync.dma_start(out=q_sb[b][:], in_=query_layer[b].rearrange("h (p j) d -> p h (j d)", j=NT))
 
+        def load_q_part(h0, h1):
+            if h0 == 0:
+                q_sb[0] = loads.tile([P, H, NT * D], BF16, name="q_sb", tag="q_sb")
+            nc.sync.dma_start(
+                out=q_sb[0][:, h0:h1, :], in_=query_layer[0, h0:h1].rearrange("h (p j) d -> p h (j d)", j=NT)
+            )
+
         def load_v(b):
             if b >= B:
                 return
@@ -76,8 +83,8 @@ def tile_selfattention_t_kernel(tc, query_layer, key_layer, value_layer, attenti
                 in_=value_layer[b].rearrange("g (u p e) d -> p (g u) (e d)", u=2, e=2),
             )
 
-        def prep_pe(b, i):
-            pt = ps_p.tile([P, 2, NT, P], BF16, name="prep", tag="prep")
+        def prep_pe(b, i, pool=None, tag="prep"):
+            pt = (ps_p if pool is None else pool).tile([P, 2, NT, P], BF16, name="prep", tag=tag)
             prep[(b, i)] = pt
             for a in range(2):
                 for j in range(NT if i == 0 else NM):
@@ -116,8 +123,8 @@ def tile_selfattention_t_kernel(tc, query_layer, key_layer, value_layer, attenti
                 out=vc[b][:].bitcast(FP8X4), scales=vs[b][:], in_=vg[:].rearrange("p g d t -> p (g d t)")
             )
 
-        def qt_pe(n):
-            pt = ps_p.tile([P, 2, NT, P], BF16, name="prep", tag="prep")
+        def qt_pe(n, pool=None, tag="prep"):
+            pt = (ps_p if pool is None else pool).tile([P, 2, NT, P], BF16, name="prep", tag=tag)
             prep[("q", n)] = pt
             for a in range(2):
                 for j in range(NT):
@@ -143,8 +150,8 @@ def tile_selfattention_t_kernel(tc, query_layer, key_layer, value_layer, attenti
             if hn % 2 == 1:
                 if m + 1 < NH:
                     qt_pe(m + 1)
-            elif b + 1 < B and hn // 2 < 3:
-                prep_pe(b + 1, hn // 2)
+            elif b + 1 < B and hn > 0:
+                prep_pe(b + 1, hn // 2 - 1)
 
         def eva(m):
             if not live(m):
@@ -153,17 +160,19 @@ def tile_selfattention_t_kernel(tc, query_layer, key_layer, value_layer, attenti
             if hn % 2 == 1:
                 if m + 1 < NH:
                     qt_ev(m + 1, "S")
-            elif b + 1 < B and hn // 2 < 3:
-                prep_ev(b + 1, hn // 2, 0, "S")
+            elif b + 1 < B and hn > 0:
+                prep_ev(b + 1, hn // 2 - 1, 0, "S")
 
         def evb(m):
             if not live(m):
                 return
             b, hn = m // H, m % H
-            if hn % 2 == 0 and b + 1 < B and 1 <= hn // 2 < 3:
-                prep_ev(b + 1, hn // 2, 1, "S")
+            if hn % 2 == 0 and b + 1 < B and hn > 2:
+                prep_ev(b + 1, hn // 2 - 1, 1, "S")
 
         def pv(m):
+            if m == 0:
+                prep_v(0)
             if live(m) and m % H == 6 and m // H + 1 < B:
                 prep_v(m // H + 1)
 
@@ -294,22 +303,22 @@ def tile_selfattention_t_kernel(tc, query_layer, key_layer, value_layer, attenti
             nc.sync.dma_start(out=out[n // H, n % H].rearrange("(p j) d -> p j d", j=NT), in_=o_sb[:])
 
         load_k(0)
+        load_q_part(0, 2)
         load_m(0)
-        load_q(0)
+        load_q_part(2, H)
         load_v(0)
         load_k(1)
         load_m(1)
         prep_pe(0, 0)
+        qt_pe(0, ps_o, "o_ps")
+        prep_pe(0, 1, ps_e, "ep")
+        prep_pe(0, 2, ps_e, "ep")
         prep_ev(0, 0, 0, "S")
-        prep_pe(0, 1)
-        prep_ev(0, 1, 0, "V")
-        prep_ev(0, 1, 1, "S")
-        prep_pe(0, 2)
-        prep_ev(0, 2, 0, "V")
-        prep_ev(0, 2, 1, "S")
-        qt_pe(0)
         qt_ev(0, "V")
-        prep_v(0)
+        prep_ev(0, 1, 0, "S")
+        prep_ev(0, 1, 1, "V")
+        prep_ev(0, 2, 0, "S")
+        prep_ev(0, 2, 1, "V")
 
         for n in range(NH + 4):
             if n < NH and n % H == 0:

@@ -25,7 +25,6 @@ def tile_selfattention_t_kernel(tc, query_layer, key_layer, value_layer, attenti
     nc = tc.nc
     c = 1.0 / math.sqrt(D)
     with ExitStack() as ctx:
-        ctx.enter_context(tc.manual_schedule())
         const = ctx.enter_context(tc.tile_pool(name="const", bufs=1))
         loads = ctx.enter_context(tc.tile_pool(name="loads", bufs=2))
         batch = ctx.enter_context(tc.tile_pool(name="batch", bufs=2))

import math
from contextlib import ExitStack

import concourse.mybir as mybir
from concourse.masks import make_identity

BF16 = mybir.dt.bfloat16
F32 = mybir.dt.float32
U32 = mybir.dt.uint32
U8 = mybir.dt.uint8
FP8X4 = mybir.dt.float8_e4m3fn_x4
ALU = mybir.AluOpType
ACT = mybir.ActivationFunctionType
AX = mybir.AxisListType

B, H, G, S, D = 8, 8, 2, 512, 128
P = 128
NT = S // P
NH = B * H
NM = 3
FLOPS = 2 * 2 * B * H * S * S * D


def tile_selfattention_t_kernel(tc, query_layer, key_layer, value_layer, attention_mask, out):
    nc = tc.nc
    c = 1.0 / math.sqrt(D)
    with ExitStack() as ctx:
        const = ctx.enter_context(tc.tile_pool(name="const", bufs=1))
        loads = ctx.enter_context(tc.tile_pool(name="loads", bufs=2))
        batch = ctx.enter_context(tc.tile_pool(name="batch", bufs=2))
        work = ctx.enter_context(tc.tile_pool(name="work", bufs=2))
        ps_s = ctx.enter_context(tc.psum_pool(name="ps_s", bufs=4))
        ps_e = ctx.enter_context(tc.psum_pool(name="ps_e", bufs=2))
        ps_o = ctx.enter_context(tc.psum_pool(name="ps_o", bufs=1))
        ps_p = ctx.enter_context(tc.psum_pool(name="ps_p", bufs=1))

        ident_b = const.tile([P, P], BF16, name="ident_b")
        make_identity(nc, ident_b[:])
        ident_f = const.tile([P, P], F32, name="ident_f")
        make_identity(nc, ident_f[:])

        k_sb, m_sb, q_sb, v_sb = {}, {}, {}, {}
        kT, mt, vc, vs = {}, {}, {}, {}
        qT, sp, s_sb, e_sb, ep, grp, codes, scales = {}, {}, {}, {}, {}, {}, {}, {}
        mx, nb, nbv, rs, ri, o_ps = {}, {}, {}, {}, {}, {}
        prep = {}

        def live(n):
            return 0 <= n < NH

        def load_k(b):
            if b >= B:
                return
            k_sb[b] = loads.tile([P, G * NT, D], BF16, name="k_sb", tag="k_sb")
            nc.sync.dma_start(out=k_sb[b][:], in_=key_layer[b].rearrange("g (t p) d -> p (g t) d", p=P))

        def load_m(b):
            if b >= B:
                return
            m_sb[b] = loads.tile([P, NT, S], BF16, name="m_sb", tag="m_sb", bufs=3)
            nc.sync.dma_start(out=m_sb[b][:], in_=attention_mask[b, 0].rearrange("(p j) k -> p j k", j=NT))

        def load_q(b):
            if b >= B:
                return
            q_sb[b] = loads.tile([P, H, NT * D], BF16, name="q_sb", tag="q_sb")
            nc.sync.dma_start(out=q_sb[b][:], in_=query_layer[b].rearrange("h (p j) d -> p h (j d)", j=NT))

        def load_q_part(h0, h1):
            if h0 == 0:
                q_sb[0] = loads.tile([P, H, NT * D], BF16, name="q_sb", tag="q_sb")
            nc.sync.dma_start(
                out=q_sb[0][:, h0:h1, :], in_=query_layer[0, h0:h1].rearrange("h (p j) d -> p h (j d)", j=NT)
            )

        def load_v(b):
            if b >= B:
                return
            v_sb[b] = loads.tile([P, G * NT, D], BF16, name="v_sb", tag="v_sb")
            nc.sync.dma_start(
                out=v_sb[b][:].rearrange("p (a e) d -> p a (e d)", e=2),
                in_=value_layer[b].rearrange("g (u p e) d -> p (g u) (e d)", u=2, e=2),
            )

        def prep_pe(b, i, pool=None, tag="prep"):
            pt = (ps_p if pool is None else pool).tile([P, 2, NT, P], BF16, name="prep", tag=tag)
            prep[(b, i)] = pt
            for a in range(2):
                for j in range(NT if i == 0 else NM):
                    if i == 0:
                        src = k_sb[b][:, a * NT + j, :]
                    else:
                        kb = 2 * (i - 1) + a
                        src = m_sb[b][:, j, kb * P : (kb + 1) * P]
                    nc.tensor.transpose(out=pt[:, a, j, :], in_=src, identity=ident_b[:])

        def prep_ev(b, i, part, eng):
            pt = prep[(b, i)]
            if i == 0:
                if part == 0:
                    kT[b] = batch.tile([P, G, S], BF16, name="kT", tag="kT")
                    dst = kT[b][:].rearrange("p g s -> p (g s)")
                    src = pt[:].rearrange("p a j i -> p (a j i)")
                    nc.scalar.copy(out=dst, in_=src)
                return
            if i == 1 and part == 0:
                mt[b] = batch.tile([P, NT, NM, P], F32, name="mt", tag="mt")
            kb = 2 * (i - 1) + part
            dst = mt[b][:, kb, :, :].rearrange("p j i -> p (j i)")
            src = pt[:, part, 0:NM, :].rearrange("p j i -> p (j i)")
            if eng == "S":
                nc.scalar.mul(out=dst, in_=src, mul=math.sqrt(D))
            else:
                nc.vector.tensor_scalar_mul(out=dst, in0=src, scalar1=math.sqrt(D))

        def prep_v(b):
            vg = batch.tile([P, G, D, 4], BF16, name="vg", tag="vg", align_bytes=64)
            nc.vector.tensor_copy(out=vg[:], in_=v_sb[b][:].rearrange("p (g t) d -> p g d t", g=G))
            vc[b] = batch.tile([P, G * D], U32, name="vc", tag="vc", align_bytes=64)
            vs[b] = batch.tile([P, G * D], U8, name="vs", tag="vs", align_bytes=64)
            nc.vector.quantize_mx(
                out=vc[b][:].bitcast(FP8X4), scales=vs[b][:], in_=vg[:].rearrange("p g d t -> p (g d t)")
            )

        def qt_pe(n, pool=None, tag="prep"):
            pt = (ps_p if pool is None else pool).tile([P, 2, NT, P], BF16, name="prep", tag=tag)
            prep[("q", n)] = pt
            for a in range(2):
                for j in range(NT):
                    nc.tensor.transpose(
                        out=pt[:, a, j, :],
                        in_=q_sb[(n + a) // H][:, (n + a) % H, j * D : (j + 1) * D],
                        identity=ident_b[:],
                    )

        def qt_ev(n, eng):
            qT[n // 2] = work.tile([P, 2, NT, P], BF16, name="qT", tag="qT", bufs=3)
            dst = qT[n // 2][:].rearrange("p a j i -> p (a j i)")
            src = prep[("q", n)][:].rearrange("p a j i -> p (a j i)")
            if eng == "S":
                nc.scalar.copy(out=dst, in_=src)
            else:
                nc.vector.tensor_copy(out=dst, in_=src)

        def bf(m):
            if not live(m):
                return
            b, hn = m // H, m % H
            if hn % 2 == 1:
                if m + 1 < NH:
                    qt_pe(m + 1)
            elif b + 1 < B and hn > 0:
                prep_pe(b + 1, hn // 2 - 1)

        def eva(m):
            if not live(m):
                return
            b, hn = m // H, m % H
            if hn % 2 == 1:
                if m + 1 < NH:
                    qt_ev(m + 1, "S")
            elif b + 1 < B and hn > 0:
                prep_ev(b + 1, hn // 2 - 1, 0, "S")

        def evb(m):
            if not live(m):
                return
            b, hn = m // H, m % H
            if hn % 2 == 0 and b + 1 < B and hn > 2:
                prep_ev(b + 1, hn // 2 - 1, 1, "S")

        def pv(m):
            if m == 0:
                prep_v(0)
            if live(m) and m % H == 6 and m // H + 1 < B:
                prep_v(m // H + 1)

        def qk(n, j):
            if not live(n):
                return
            t = n * NT + j
            b, h = n // H, n % H
            sp[t] = ps_s.tile([P, S], F32, name="sp", tag="sp")
            nc.tensor.matmul(
                out=sp[t][:], lhsT=qT[n // 2][:, n % 2, j, :], rhs=kT[b][:, h // (H // G), :], start=True, stop=(j >= NM)
            )

        def ta(n, j):
            if not live(n):
                return
            t = n * NT + j
            for kb in range(NT):
                nc.tensor.matmul(
                    out=sp[t][:, kb * P : (kb + 1) * P],
                    lhsT=mt[n // H][:, kb, j, :],
                    rhs=ident_f[:],
                    start=False,
                    stop=(kb == NT - 1),
                    is_transpose=True,
                )

        def stt(n, j):
            if not live(n):
                return
            t = n * NT + j
            s_sb[t] = work.tile([P, S], F32, name="s_sb", tag="s_sb", bufs=4)
            nc.vector.scalar_tensor_tensor(
                out=s_sb[t][:], in0=sp[t][:], scalar=c, in1=m_sb[n // H][:, j, :], op0=ALU.mult, op1=ALU.add
            )

        def red(n, j):
            if not live(n):
                return
            t = n * NT + j
            if j >= NM:
                nbv[t] = work.tile([P, 1], F32, name="nbv", tag="nbv", bufs=6)
                nc.vector.tensor_reduce(out=nbv[t][:], in_=s_sb[t][:], axis=AX.X, op=ALU.max, negate=True)
                return
            if n not in mx:
                mx[n] = work.tile([P, NT], F32, name="mx", tag="mx", bufs=4)
                nb[n] = work.tile([P, NT], F32, name="nb", tag="nb", bufs=4)
            nc.vector.tensor_reduce(out=mx[n][:, j : j + 1], in_=sp[t][:], axis=AX.X, op=ALU.max)
            nc.gpsimd.tensor_scalar(
                out=nb[n][:, j : j + 1], in0=mx[n][:, j : j + 1], scalar1=-c, scalar2=0.0, op0=ALU.mult, op1=ALU.add
            )

        def ex(n, j):
            if not live(n):
                return
            t = n * NT + j
            if n not in rs:
                rs[n] = work.tile([P, NT], F32, name="rs", tag="rs", bufs=8)
            e_sb[t] = work.tile([P, S], BF16, name="e_sb", tag="e_sb", bufs=16)
            if j >= NM:
                scores, factor, bias = s_sb[t], 1.0, nbv[t][:]
            else:
                scores, factor, bias = sp[t], c, nb[n][:, j : j + 1]
            nc.scalar.activation(
                out=e_sb[t][:], in_=scores[:], func=ACT.Exp, bias=bias, scale=factor, accum_out=rs[n][:, j : j + 1]
            )

        def te(n, a):
            if not live(n):
                return
            r = 2 * n + a
            ep[r] = ps_e.tile([P, 2, 2, P], F32, name="ep", tag="ep")
            for i in range(2):
                for u in range(2):
                    nc.tensor.transpose(
                        out=ep[r][:, i, u, :],
                        in_=e_sb[2 * r + i][:].bitcast(F32)[:, u * P : (u + 1) * P],
                        identity=ident_f[:],
                    )

        def cp(n, a):
            if not live(n):
                return
            r = 2 * n + a
            grp[r] = work.tile([P, 2, P, 4], BF16, name="grp", tag="grp", bufs=8, align_bytes=64)
            nc.scalar.copy(out=grp[r][:].bitcast(F32), in_=ep[r][:].rearrange("p a u i -> p a i u"))

        def qz(n, a):
            if not live(n):
                return
            r = 2 * n + a
            codes[r] = work.tile([P, 2 * P], U32, name="codes", tag="codes", bufs=12, align_bytes=64)
            scales[r] = work.tile([P, 2 * P], U8, name="scales", tag="scales", bufs=12, align_bytes=64)
            nc.vector.quantize_mx(
                out=codes[r][:].bitcast(FP8X4), scales=scales[r][:], in_=grp[r][:].rearrange("p a i t -> p (a i t)")
            )

        def mm(n):
            if not live(n):
                return
            b, g = n // H, (n % H) // (H // G)
            o_ps[n] = ps_o.tile([P, NT, D], F32, name="o_ps", tag="o_ps")
            for j in range(NT):
                r, a = 2 * n + j // 2, j % 2
                nc.tensor.matmul_mx(
                    out=o_ps[n][:, j, :],
                    lhsT=codes[r][:, a * P : (a + 1) * P].bitcast(FP8X4),
                    lhsT_scale=scales[r][:, a * P : (a + 1) * P],
                    rhs=vc[b][:, g * D : (g + 1) * D].bitcast(FP8X4),
                    rhs_scale=vs[b][:, g * D : (g + 1) * D],
                    start=True,
                    stop=True,
                )

        def rc(n):
            if not live(n):
                return
            ri[n] = work.tile([P, NT], F32, name="ri", tag="ri", bufs=4)
            nc.vector.reciprocal(out=ri[n][:], in_=rs[n][:])

        def ov(n):
            if not live(n):
                return
            o_sb = work.tile([P, NT, D], F32, name="o_sb", tag="o_sb", bufs=4)
            nc.vector.tensor_tensor(
                out=o_sb[:], in0=o_ps[n][:], in1=ri[n][:].unsqueeze(2).to_broadcast([P, NT, D]), op=ALU.mult
            )
            nc.sync.dma_start(out=out[n // H, n % H].rearrange("(p j) d -> p j d", j=NT), in_=o_sb[:])

        load_k(0)
        load_q_part(0, 2)
        load_m(0)
        load_q_part(2, H)
        load_v(0)
        load_k(1)
        load_m(1)
        prep_pe(0, 0)
        qt_pe(0, ps_o, "o_ps")
        prep_pe(0, 1, ps_e, "ep")
        prep_pe(0, 2, ps_e, "ep")
        prep_ev(0, 0, 0, "S")
        qt_ev(0, "V")
        prep_ev(0, 1, 0, "S")
        prep_ev(0, 1, 1, "V")
        prep_ev(0, 2, 0, "S")
        prep_ev(0, 2, 1, "V")

        for n in range(NH + 4):
            if n < NH and n % H == 0:
                load_q(n // H + 1)
                load_v(n // H + 1)
                load_k(n // H + 2)
                load_m(n // H + 2)
            te(n - 2, 1)
            cp(n - 2, 0)
            red(n - 1, 2)
            qz(n - 3, 0)
            red(n - 1, 3)
            pv(n - 1)
            ex(n - 1, 1)
            cp(n - 2, 1)
            bf(n)
            ex(n - 1, 2)
            qk(n, 0)
            ta(n, 0)
            qk(n, 3)
            mm(n - 4)
            ex(n - 1, 3)
            red(n, 0)
            stt(n, 3)
            qk(n, 1)
            ta(n, 1)
            qz(n - 3, 1)
            red(n, 1)
            te(n - 1, 0)
            eva(n)
            qk(n, 2)
            evb(n)
            ta(n, 2)
            ov(n - 4)
            rc(n - 2)
            ex(n, 0)
